import numpy as np
import ml_dtypes


def mxq(x, axis, fmt="e4m3"):
    dtype, down = {"e4m3": (ml_dtypes.float8_e4m3fn, 7), "e5m2": (ml_dtypes.float8_e5m2, 14)}[fmt]
    v = np.moveaxis(np.asarray(x, np.float32).astype(ml_dtypes.bfloat16).astype(np.float64), axis, -1)
    blocks = v.reshape(v.shape[:-1] + (-1, 32))
    amax = np.abs(blocks).max(-1, keepdims=True)
    byte = np.maximum(np.where(amax > 0, np.frexp(amax)[1] - 1 + 127, 0) - down, 1)
    scale = np.exp2(byte - 127.0)
    codes = (blocks / scale).astype(np.float32).astype(dtype).astype(np.float64)
    return np.moveaxis((codes * scale).reshape(v.shape), -1, axis)


WIDE = False


def mx_kscale(k):
    if not WIDE:
        return np.ones(k)
    levels = np.array([18, -18])
    if k % 512:
        return np.exp2(np.random.permutation(np.resize(levels, k // 32))).repeat(32)
    a = np.empty((k // 512, 16))
    for p in range(k // 512):
        a[p, :8] = np.random.permutation(np.resize(levels, 8))
        for g in range(8):
            far = levels[np.abs(levels - a[p, g]) >= 10]
            a[p, g + 8] = far[np.random.randint(len(far))]
    return np.exp2(a.ravel()).repeat(32)


BF16 = ml_dtypes.bfloat16


def bf(x):
    return np.asarray(x, np.float32).astype(BF16)


def f64(x):
    return np.asarray(x).astype(np.float64)


B, DIM = 1024, 512
K = 2 * DIM
GATES = ("i", "f", "o", "z")


def sigmoid(v):
    return 1.0 / (1.0 + np.exp(-v))


def setup_inputs():
    s = mx_kscale(B)[:, None]
    u = mx_kscale(4 * DIM).reshape(4, DIM)[:, : DIM // 4].ravel()

    x0 = bf(np.random.standard_normal((B, DIM)))
    h0 = bf(np.random.standard_normal((B, DIM)))
    c = bf(np.random.standard_normal((B, DIM)))
    n = bf(0.5 + np.random.uniform(0.0, 1.0, (B, DIM)))
    m0 = bf(np.random.standard_normal((B, DIM)))
    w0 = {}
    b = {}
    for g in GATES:
        w0[g] = bf(np.random.standard_normal((DIM, K)) / np.sqrt(K))
        b[g] = bf(np.random.standard_normal(DIM) * 0.2)
    g_out = np.random.standard_normal((4, B, DIM)) * np.exp2(np.random.randint(-6, 1, (1, B, 1))) * 4.0

    combined = np.concatenate([f64(x0), f64(h0)], axis=-1)
    W = np.concatenate([f64(w0[g]) for g in GATES], axis=0)
    bias = np.concatenate([f64(b[g]) for g in GATES], axis=0)
    gates = combined @ W.T + bias

    gap = gates[:, DIM : 2 * DIM] + f64(m0) - gates[:, :DIM]
    m = bf(np.where(np.abs(gap) < 1.0 / 64.0, f64(m0) + 0.125, f64(m0)))

    inp = {}
    inp["x"] = bf(f64(x0) * s)
    inp["h"] = bf(f64(h0) * s)
    inp["c"] = c
    inp["n"] = n
    inp["m"] = m
    for g in GATES:
        inp["W_" + g] = bf(f64(w0[g]) / u[:, None])
        inp["b_" + g] = b[g]
    inp["gates"] = np.asarray(gates, np.float32)
    inp["grad_out"] = bf(g_out / s[None] * u)
    return inp


def reference(x, h, c, n, m, W_i, b_i, W_f, b_f, W_o, b_o, W_z, b_z, gates, grad_out):
    c, n, m = f64(c), f64(n), f64(m)
    i_t, f_t, o_t, z_t = np.split(f64(gates), 4, axis=-1)
    gh, gc, gn, gm = f64(grad_out)
    a = f_t + m
    m_new = np.maximum(a, i_t)
    i = np.exp(i_t - m_new)
    f = np.exp(a - m_new)
    z = np.tanh(z_t)
    o = sigmoid(o_t)
    r = 1.0 / (f * n + i + 1e-6)
    q = (f * c + i * z) * r
    dc = gc + gh * o * r
    dn = gn - gh * o * q * r
    p_i = (dc * z + dn) * i
    p_f = (dc * c + dn * n) * f
    d_i = np.where(a > i_t, p_i, gm - p_f)
    d_f = np.where(a > i_t, gm - p_i, p_f)
    d_o = gh * q * o * (1.0 - o)
    d_z = dc * i * (1.0 - z * z)
    dgates = np.concatenate([d_i, d_f, d_o, d_z], axis=-1)
    Wx = np.concatenate([f64(W_i)[:, :DIM], f64(W_f)[:, :DIM], f64(W_o)[:, :DIM], f64(W_z)[:, :DIM]], axis=0)
    combined = np.concatenate([f64(x), f64(h)], axis=-1)
    dx = mxq(dgates, 1, "e5m2") @ mxq(Wx, 0, "e4m3")
    dW_f = mxq(d_f, 0, "e5m2").T @ mxq(combined, 0, "e4m3")
    return dx, dW_f

@@ -1,0 +1,377 @@
+from contextlib import ExitStack
+
+import concourse.mybir as mybir
+from concourse.masks import make_identity
+
+B, DIM = 1024, 512
+FLOPS = 2 * B * 4 * DIM * DIM + 2 * B * DIM * 2 * DIM
+BYTES = B * 4 * DIM * 4 + 4 * B * DIM * 2 + 5 * B * DIM * 2 + 4 * DIM * DIM * 2 + 2 * B * DIM * 4
+
+F32 = mybir.dt.float32
+BF16 = mybir.dt.bfloat16
+U32 = mybir.dt.uint32
+U8 = mybir.dt.uint8
+E4M3 = mybir.dt.float8_e4m3fn_x4
+E5M2 = mybir.dt.float8_e5m2_x4
+ALU = mybir.AluOpType
+ACT = mybir.ActivationFunctionType
+
+P = 128
+PACK = 4
+CHUNKS = 8
+EPS = 1e-6
+
+
+def tile_slstmcell_v_kernel(tc, x, h, c, n, m, W_i, b_i, W_f, b_f, W_o, b_o, W_z, b_z,
+                                        gates, grad_out, out_0, out_1):
+    nc = tc.nc
+    vec, act, pe, dma = nc.vector, nc.scalar, nc.tensor, nc.sync
+
+    def rows(ap, k):
+        return ap.rearrange("(g p j) w -> g j p w", g=2, j=PACK)[k // PACK, k % PACK]
+
+    grad_rows = grad_out.rearrange("s (g p j) w -> g j p s w", g=2, j=PACK)
+    out_1_rows = out_1.rearrange("(p t) w -> t p w", t=PACK)
+    sources = [w[:, 0:DIM] for w in (W_i, W_f, W_o, W_z)]
+    sources = sources + [x[0:512, :], h[0:512, :], x[512:1024, :], h[512:1024, :]]
+
+    with ExitStack() as ctx:
+        sb = ctx.enter_context(tc.tile_pool(name="sb", bufs=1))
+        ps = ctx.enter_context(tc.psum_pool(name="ps", bufs=1))
+        ctx.enter_context(tc.manual_schedule())
+
+        T = {}
+
+        def new(name, k, bufs, shape=(P, DIM), dtype=F32):
+            T[name, k] = sb.tile(list(shape), dtype, name=name, tag=name, bufs=bufs, align_bytes=64)
+            return T[name, k]
+
+        def bank(tag, key, shape=(P, DIM)):
+            T[key] = ps.tile(list(shape), F32, name=tag, tag=tag)
+            return T[key]
+
+        def tt(out, in0, in1, op):
+            vec.tensor_tensor(out=out, in0=in0, in1=in1, op=op)
+
+        def stt(out, in0, scalar, in1, op0, op1):
+            vec.scalar_tensor_tensor(out=out, in0=in0, scalar=scalar, in1=in1, op0=op0, op1=op1)
+
+        def sorted_cols(tile):
+            return tile[:].rearrange("p (t q) -> p q t", t=PACK)
+
+        def natural_cols(ap):
+            return ap.rearrange("p (q t) -> p q t", t=PACK)
+
+        def load_a(k):
+            dma.dma_start(out=new("m", k, 3, dtype=BF16)[:], in_=rows(m, k))
+            dma.dma_start(out=new("gif", k, 3, shape=(P, 2 * DIM))[:], in_=rows(gates, k)[:, 0:2 * DIM])
+            dma.dma_start(out=new("gz", k, 2)[:], in_=rows(gates, k)[:, 3 * DIM:4 * DIM])
+            dma.dma_start(out=new("n", k, 3, dtype=BF16)[:], in_=rows(n, k))
+            dma.dma_start(out=new("c", k, 3, dtype=BF16)[:], in_=rows(c, k))
+
+        def load_b(k):
+            dma.dma_start(out=new("ot", k, 3)[:], in_=rows(gates, k)[:, 2 * DIM:3 * DIM])
+            dma.dma_start(out=new("grad", k, 3, shape=(P, 4, DIM), dtype=BF16)[:],
+                          in_=grad_rows[k // PACK, k % PACK])
+
+        def load_raw(s):
+            dma.dma_start(out=new("raw", s, 2, shape=(P, PACK, DIM), dtype=BF16)[:],
+                          in_=sources[s].rearrange("(p j) w -> p j w", j=PACK))
+
+        def interleave(s):
+            grouped = new("grouped", s, 1, shape=(P, DIM, PACK), dtype=BF16)
+            act.copy(out=grouped[:].rearrange("p (c i) t -> p c t i", i=4),
+                     in_=T["raw", s][:].rearrange("p t (c i) -> p c t i", i=4))
+
+        def quantize_raw(s):
+            codes = new("e4_codes", s, 8, dtype=U32)
+            scales = new("e4_scales", s, 8, dtype=U8)
+            vec.quantize_mx(out=codes[:].bitcast(E4M3), scales=scales[:],
+                            in_=T["grouped", s][:].rearrange("p w j -> p (w j)"))
+
+        def pre_t(k):
+            tt(new("d", k, 6)[:], T["m", k][:], T["gif", k][:, 0:DIM], ALU.subtract)
+
+        def pre_d(k):
+            tt(T["d", k][:], T["d", k][:], T["gif", k][:, DIM:2 * DIM], ALU.add)
+
+        def s1(k):
+            z, jn, i, f, d = new("z", k, 2), new("jn", k, 6), new("i", k, 2), new("f", k, 2), T["d", k]
+            act.activation(out=z[:], in_=T["gz", k][:], func=ACT.Tanh)
+            act.activation(out=f[:], in_=d[:], func=ACT.Relu, scale=-1.0)
+            act.activation(out=i[:], in_=d[:], func=ACT.Relu)
+            act.activation(out=f[:], in_=f[:], func=ACT.Exp, scale=-1.0)
+            act.activation(out=i[:], in_=i[:], func=ACT.Exp, scale=-1.0)
+            act.activation(out=jn[:], in_=z[:], func=ACT.Square)
+
+        def a_first(k, ahead):
+            fn, fc, iz = new("fn", k, 1), new("fc", k, 1), new("iz", k, 1)
+            D, N = new("D", k, 5), new("N", k, 5)
+            if ahead:
+                pre_t(k + 1)
+            tt(fn[:], T["f", k][:], T["n", k][:], ALU.mult)
+            if ahead:
+                pre_d(k + 1)
+            tt(fc[:], T["f", k][:], T["c", k][:], ALU.mult)
+            tt(iz[:], T["i", k][:], T["z", k][:], ALU.mult)
+            tt(D[:], fn[:], T["i", k][:], ALU.add)
+            tt(N[:], fc[:], iz[:], ALU.add)
+
+        def a_second(k):
+            U, V, d = new("U", k, 5), new("V", k, 5), T["d", k]
+            stt(V[:], d[:], 0.0, T["D", k][:], ALU.is_gt, ALU.mult)
+            stt(U[:], d[:], 0.0, T["N", k][:], ALU.is_gt, ALU.mult)
+            tt(V[:], T["fn", k][:], V[:], ALU.subtract)
+            tt(U[:], T["fc", k][:], U[:], ALU.subtract)
+            stt(T["jn", k][:], T["jn", k][:], 1.0, T["i", k][:], ALU.subtract, ALU.mult)
+
+        def s_abs(k):
+            act.activation(out=new("r2", k, 5)[:], in_=T["D", k][:], func=ACT.Abs, bias=EPS)
+
+        def s_ln(k):
+            act.activation(out=T["r2", k][:], in_=T["r2", k][:], func=ACT.Ln)
+
+        def s2(k):
+            act.activation(out=T["r2", k][:], in_=T["r2", k][:], func=ACT.Exp, scale=-2.0)
+            act.activation(out=new("th", k, 2)[:], in_=T["ot", k][:], func=ACT.Tanh, scale=0.5)
+            act.activation(out=sorted_cols(new("gmn", k, 2)), in_=natural_cols(T["grad", k][:, 3, :]),
+                           func=ACT.Copy, scale=-1.0)
+
+        def v_go(k):
+            stt(new("g2", k, 1)[:], T["th", k][:], 1.0, T["grad", k][:, 0, :], ALU.add, ALU.mult)
+
+        def add_blocks(key, tile, start=False, stop=False):
+            for t in range(PACK):
+                cols = slice(t * P, (t + 1) * P)
+                pe.matmul(T[key][:, cols], lhsT=tile[:, cols], rhs=ident[:], is_transpose=True,
+                          start=start and t == 0, stop=stop and t == PACK - 1)
+
+        def b_first(k):
+            g2, grad, D, N = T["g2", k], T["grad", k], T["D", k], T["N", k]
+            G, H, dn, M2 = new("G", k, 1), new("H", k, 1), new("dn", k, 1), new("M2", k, 2)
+            stt(g2[:], g2[:], 0.5, T["r2", k][:], ALU.mult, ALU.mult)
+            stt(sorted_cols(M2), natural_cols(T["d", k][:]), 0.0, natural_cols(grad[:, 3, :]), ALU.is_gt, ALU.mult)
+            stt(G[:], D[:], EPS, g2[:], ALU.add, ALU.mult)
+            stt(dn[:], g2[:], -1.0, N[:], ALU.mult, ALU.mult)
+            stt(H[:], G[:], -0.5, N[:], ALU.mult, ALU.mult)
+            tt(dn[:], dn[:], grad[:, 2, :], ALU.add)
+            tt(G[:], G[:], grad[:, 1, :], ALU.add)
+
+        def b_second(k):
+            dc, dn = T["G", k], T["dn", k]
+            t1, t2 = new("t1", k, 2), new("t2", k, 2)
+            doz = new("doz", k, 2, shape=(P, 2, DIM), dtype=BF16)
+            bank("sum_f", ("sum_f", k))
+            bank("sum_i", ("sum_i", k))
+            add_blocks(("sum_f", k), T["M2", k], start=True)
+            add_blocks(("sum_i", k), T["gmn", k], start=True)
+            add_blocks(("sum_i", k), T["M2", k])
+            tt(sorted_cols(t2), natural_cols(dn[:]), natural_cols(T["V", k][:]), ALU.mult)
+            add_blocks(("sum_f", k), t2)
+            add_blocks(("sum_i", k), t2)
+            tt(sorted_cols(t1), natural_cols(dc[:]), natural_cols(T["U", k][:]), ALU.mult)
+            add_blocks(("sum_f", k), t1, stop=True)
+            add_blocks(("sum_i", k), t1, stop=True)
+            stt(doz[:, 0, :], T["th", k][:], 1.0, T["H", k][:], ALU.subtract, ALU.mult)
+            stt(doz[:, 1, :], dc[:], -1.0, T["jn", k][:], ALU.mult, ALU.mult)
+            oz = bank("oz", ("oz", k), shape=(P, 2, 2, P))
+            for g in range(2):
+                words = doz[:, g, :].bitcast(F32)
+                for u in range(2):
+                    pe.transpose(oz[:, g, u, :], words[:, u:2 * P:2], ident[:])
+
+        def copy_f(k):
+            dT = new("dT", k, 2, shape=(P, 4, DIM), dtype=BF16)
+            act.copy(out=dT[:, 1, :].rearrange("p (r t) -> p r t", t=PACK),
+                     in_=T["sum_f", k][:].rearrange("p (t r) -> p r t", t=PACK))
+            words = dT[:, 1, :].bitcast(F32)
+            for u in range(2):
+                if k % PACK == 0:
+                    bank("back%d" % u, ("back", k // PACK, u), shape=(P, PACK, P))
+                pe.transpose(T["back", k // PACK, u][:, k % PACK, :], words[:, u:2 * P:2], ident[:])
+
+        def copy_i(k):
+            act.activation(out=T["dT", k][:, 0, :].rearrange("p (r t) -> p r t", t=PACK),
+                           in_=T["sum_i", k][:].rearrange("p (t r) -> p r t", t=PACK),
+                           func=ACT.Copy, scale=-1.0)
+
+        def copy_oz(k):
+            words = T["dT", k][:, 2:4, :].rearrange("p g w -> p (g w)").bitcast(F32)
+            act.copy(out=words.rearrange("p (g r u) -> p g r u", g=2, u=2),
+                     in_=T["oz", k][:].rearrange("p g u r -> p g r u"))
+
+        def copies(k):
+            copy_f(k)
+            copy_i(k)
+            copy_oz(k)
+
+        def product_0(k):
+            codes, scales = new("d_codes", k, 2, dtype=U32), new("d_scales", k, 2, dtype=U8)
+            vec.quantize_mx(out=codes[:].bitcast(E5M2), scales=scales[:],
+                            in_=T["dT", k][:].rearrange("p g w -> p (g w)"))
+            acc = bank("acc0", ("acc0", k))
+            for g in range(4):
+                cols = slice(g * P, (g + 1) * P)
+                pe.matmul_mx(out=acc[:], lhsT=codes[:, cols].bitcast(E5M2), lhsT_scale=scales[:, cols],
+                             rhs=T["e4_codes", g][:].bitcast(E4M3), rhs_scale=T["e4_scales", g][:],
+                             start=g == 0, stop=g == 3)
+
+        def store_0(k):
+            res = new("res", ("o0", k), 3)
+            act.copy(out=res[:], in_=T["acc0", k][:])
+            dma.dma_start(out=rows(out_0, k), in_=res[:])
+
+        def back_copy(g, u, copy):
+            dfa = new("dfa%d" % u, g, 1, shape=(P, 2 * DIM), dtype=BF16)
+            halves = T["back", g, u][:].rearrange("r j p -> r (j p)").bitcast(BF16)
+            copy(out=dfa[:].rearrange("r (e p j) -> r e p j", e=2, j=PACK),
+                 in_=halves.rearrange("r (j p e) -> r e p j", j=PACK, e=2))
+
+        def quantize_back(g, u):
+            codes = new("f_codes", (g, u), 4, shape=(P, 2 * P), dtype=U32)
+            scales = new("f_scales", (g, u), 4, shape=(P, 2 * P), dtype=U8)
+            vec.quantize_mx(out=codes[:].bitcast(E5M2), scales=scales[:], in_=T["dfa%d" % u, g][:])
+
+        def pass_1(t, half, g, tag=None):
+            if g == 0:
+                bank(tag, ("acc1", t, half))
+            cols = slice((t % 2) * P, (t % 2 + 1) * P)
+            s = 4 + 2 * g + half
+            pe.matmul_mx(out=T["acc1", t, half][:],
+                         lhsT=T["f_codes", (g, t // 2)][:, cols].bitcast(E5M2),
+                         lhsT_scale=T["f_scales", (g, t // 2)][:, cols],
+                         rhs=T["e4_codes", s][:].bitcast(E4M3), rhs_scale=T["e4_scales", s][:],
+                         start=g == 0, stop=g == 1)
+
+        def store_1(t, half, copy):
+            res = new("res", ("o1", t, half), 3)
+            copy(out=res[:], in_=T["acc1", t, half][:])
+            dma.dma_start(out=out_1_rows[t][:, half * DIM:(half + 1) * DIM], in_=res[:])
+
+        load_a(0)
+        load_a(1)
+        warm = new("warm", 0, 1, shape=(P, 1))
+        vec.memset(warm[:], 0.0)
+        act.activation(out=warm[:], in_=warm[:], func=ACT.Exp)
+        ident = new("ident", 0, 1, shape=(P, P))
+        make_identity(nc, ident[:])
+        load_raw(0)
+        pre_t(0)
+        pre_d(0)
+        s1(0)
+        load_a(2)
+        pre_t(1)
+        pre_d(1)
+        s1(1)
+
+        for k in range(5):
+            if k >= 1:
+                load_a(k + 2)
+            if k < 3:
+                load_raw(k + 1)
+            if k >= 2:
+                load_b(k - 2)
+            a_first(k, ahead=k >= 1)
+            if k == 4:
+                s2(0)
+            if k >= 1:
+                s1(k + 1)
+            if k == 3:
+                s_ln(0)
+                s_ln(1)
+                s_ln(2)
+            s_abs(k)
+            if k == 3:
+                s_ln(3)
+            if 1 <= k <= 3:
+                quantize_raw(k - 1)
+            a_second(k)
+            if k < 3:
+                interleave(k)
+        v_go(0)
+
+        for k in range(CHUNKS):
+            if 1 <= k <= 5:
+                load_b(k + 2)
+            if k <= 3:
+                load_raw(k + 4)
+            if k + 1 < CHUNKS:
+                s2(k + 1)
+            b_first(k)
+            if 1 <= k <= 3:
+                store_0(k - 1)
+            if k >= 4:
+                copies(k - 1)
+            if k >= 5:
+                store_0(k - 2)
+            if k == 4:
+                back_copy(0, 0, act.copy)
+                back_copy(0, 1, act.copy)
+            s = {0: 3, 1: 4, 2: 5, 3: 6, 5: 7}.get(k)
+            if s is not None:
+                interleave(s)
+            b_second(k)
+            if k + 1 < CHUNKS:
+                v_go(k + 1)
+            if k >= 4:
+                product_0(k - 1)
+            if k == 5:
+                quantize_back(0, 0)
+                quantize_back(0, 1)
+            if s is not None:
+                quantize_raw(s)
+            if k == 6:
+                pass_1(2, 0, 0, "acc1a")
+                pass_1(2, 1, 0, "acc1b")
+            if k < 3:
+                a = k + 5
+                if a == 5:
+                    load_a(7)
+                a_first(a, ahead=a < 7)
+                if a < 7:
+                    s1(a + 1)
+                    copies(k)
+                    s_abs(a)
+                else:
+                    s_ln(4)
+                    s_ln(5)
+                    copies(k)
+                    s_ln(6)
+                    s_abs(7)
+                    s_ln(7)
+                a_second(a)
+                product_0(k)
+
+        last = CHUNKS - 1
+        copy_f(last)
+        copy_i(last)
+        pass_1(3, 0, 0, "sum_f")
+        pass_1(3, 1, 0, "sum_i")
+        back_copy(1, 1, vec.tensor_copy)
+        back_copy(1, 0, act.copy)
+        copy_oz(last)
+        store_0(last - 1)
+        pass_1(0, 0, 0, "oz")
+        pass_1(0, 1, 0, "back1")
+        quantize_back(1, 1)
+        pass_1(1, 0, 0, "back0")
+        quantize_back(1, 0)
+        pass_1(2, 0, 1)
+        pass_1(2, 1, 1)
+        product_0(last)
+        pass_1(3, 0, 1)
+        pass_1(3, 1, 1)
+        pass_1(0, 0, 1)
+        pass_1(0, 1, 1)
+        pass_1(1, 0, 1)
+        store_1(2, 0, act.copy)
+        pass_1(1, 1, 0, "acc1a")
+        pass_1(1, 1, 1)
+        store_1(2, 1, vec.tensor_copy)
+        store_0(last)
+        store_1(3, 0, vec.tensor_copy)
+        store_1(3, 1, act.copy)
+        store_1(0, 0, vec.tensor_copy)
+        store_1(0, 1, act.copy)
+        store_1(1, 0, vec.tensor_copy)
+        store_1(1, 1, act.copy)

@@ -25,7 +25,7 @@ EPS = 1e-6
 def tile_slstmcell_v_kernel(tc, x, h, c, n, m, W_i, b_i, W_f, b_f, W_o, b_o, W_z, b_z,
                                         gates, grad_out, out_0, out_1):
     nc = tc.nc
-    vec, act, pe, dma = nc.vector, nc.scalar, nc.tensor, nc.sync
+    vec, act, pe, pool, dma = nc.vector, nc.scalar, nc.tensor, nc.gpsimd, nc.sync
 
     def rows(ap, k):
         return ap.rearrange("(g p j) w -> g j p w", g=2, j=PACK)[k // PACK, k % PACK]
@@ -62,26 +62,31 @@ def tile_slstmcell_v_kernel(tc, x, h, c, n, m, W_i, b_i, W_f, b_f, W_o, b_o, W_z
         def natural_cols(ap):
             return ap.rearrange("p (q t) -> p q t", t=PACK)
 
+        def load_d(k):
+            dma.dma_start(out=new("gif", k, 2, shape=(P, 2 * DIM))[:], in_=rows(gates, k)[:, 0:2 * DIM])
+            dma.dma_start(out=new("m", k, 2, dtype=BF16)[:], in_=rows(m, k))
+
         def load_a(k):
-            dma.dma_start(out=new("m", k, 3, dtype=BF16)[:], in_=rows(m, k))
-            dma.dma_start(out=new("gif", k, 3, shape=(P, 2 * DIM))[:], in_=rows(gates, k)[:, 0:2 * DIM])
+            dma.dma_start(out=new("c", k, 3, dtype=BF16)[:], in_=rows(c, k))
             dma.dma_start(out=new("gz", k, 2)[:], in_=rows(gates, k)[:, 3 * DIM:4 * DIM])
             dma.dma_start(out=new("n", k, 3, dtype=BF16)[:], in_=rows(n, k))
-            dma.dma_start(out=new("c", k, 3, dtype=BF16)[:], in_=rows(c, k))
+            dma.dma_start(out=new("gm", k, 8, dtype=BF16)[:], in_=grad_rows[k // PACK, k % PACK][:, 3, :])
 
         def load_b(k):
             dma.dma_start(out=new("ot", k, 3)[:], in_=rows(gates, k)[:, 2 * DIM:3 * DIM])
-            dma.dma_start(out=new("grad", k, 3, shape=(P, 4, DIM), dtype=BF16)[:],
-                          in_=grad_rows[k // PACK, k % PACK])
+            dma.dma_start(out=new("grad", k, 3, shape=(P, 3, DIM), dtype=BF16)[:],
+                          in_=grad_rows[k // PACK, k % PACK][:, 0:3, :])
 
         def load_raw(s):
             dma.dma_start(out=new("raw", s, 2, shape=(P, PACK, DIM), dtype=BF16)[:],
                           in_=sources[s].rearrange("(p j) w -> p j w", j=PACK))
 
-        def interleave(s):
-            grouped = new("grouped", s, 1, shape=(P, DIM, PACK), dtype=BF16)
-            act.copy(out=grouped[:].rearrange("p (c i) t -> p c t i", i=4),
-                     in_=T["raw", s][:].rearrange("p t (c i) -> p c t i", i=4))
+        def interleave(s, copy, half=None):
+            if half != 1:
+                new("grouped", s, 1, shape=(P, DIM, PACK), dtype=BF16)
+            cols = slice(0, DIM) if half is None else slice(half * DIM // 2, (half + 1) * DIM // 2)
+            copy(out=T["grouped", s][:, cols, :].rearrange("p (c i) t -> p c t i", i=4),
+                 in_=T["raw", s][:, :, cols].rearrange("p t (c i) -> p c t i", i=4))
 
         def quantize_raw(s):
             codes = new("e4_codes", s, 8, dtype=U32)
@@ -89,41 +94,68 @@ def tile_slstmcell_v_kernel(tc, x, h, c, n, m, W_i, b_i, W_f, b_f, W_o, b_o, W_z
             vec.quantize_mx(out=codes[:].bitcast(E4M3), scales=scales[:],
                             in_=T["grouped", s][:].rearrange("p w j -> p (w j)"))
 
-        def pre_t(k):
-            tt(new("d", k, 6)[:], T["m", k][:], T["gif", k][:, 0:DIM], ALU.subtract)
+        def pre_t(k, engine):
+            T["t", k] = new("H", "t", 3) if k == 1 else X[k % 2]
+            engine.tensor_tensor(out=T["t", k][:], in0=T["m", k][:], in1=T["gif", k][:, 0:DIM], op=ALU.subtract)
 
         def pre_d(k):
-            tt(T["d", k][:], T["d", k][:], T["gif", k][:, DIM:2 * DIM], ALU.add)
+            bank("d", ("d", k))
+            add_blocks(("d", k), T["gif", k][:, DIM:2 * DIM], start=True)
+            add_blocks(("d", k), T["t", k], stop=True)
 
-        def s1(k):
-            z, jn, i, f, d = new("z", k, 2), new("jn", k, 6), new("i", k, 2), new("f", k, 2), T["d", k]
-            act.activation(out=z[:], in_=T["gz", k][:], func=ACT.Tanh)
+        def s1_gates(k):
+            i, f, rp, d = new("i", k, 1), new("f", k, 1), new("rp", k, 1), T["d", k]
             act.activation(out=f[:], in_=d[:], func=ACT.Relu, scale=-1.0)
-            act.activation(out=i[:], in_=d[:], func=ACT.Relu)
+            act.activation(out=rp[:], in_=d[:], func=ACT.Relu)
             act.activation(out=f[:], in_=f[:], func=ACT.Exp, scale=-1.0)
-            act.activation(out=i[:], in_=i[:], func=ACT.Exp, scale=-1.0)
+            act.activation(out=i[:], in_=rp[:], func=ACT.Exp, scale=-1.0)
+
+        def s1_cell(k):
+            z, jn = new("z", k, 2), new("jn", k, 6)
+            act.activation(out=z[:], in_=T["gz", k][:], func=ACT.Tanh)
             act.activation(out=jn[:], in_=z[:], func=ACT.Square)
 
-        def a_first(k, ahead):
-            fn, fc, iz = new("fn", k, 1), new("fc", k, 1), new("iz", k, 1)
-            D, N = new("D", k, 5), new("N", k, 5)
-            if ahead:
-                pre_t(k + 1)
-            tt(fn[:], T["f", k][:], T["n", k][:], ALU.mult)
-            if ahead:
-                pre_d(k + 1)
-            tt(fc[:], T["f", k][:], T["c", k][:], ALU.mult)
-            tt(iz[:], T["i", k][:], T["z", k][:], ALU.mult)
-            tt(D[:], fn[:], T["i", k][:], ALU.add)
-            tt(N[:], fc[:], iz[:], ALU.add)
+        def move(name, k):
+            bank(name + "P", (name + "P", k))
+            add_blocks((name + "P", k), T[name, k], start=True, stop=True)
 
-        def a_second(k):
-            U, V, d = new("U", k, 5), new("V", k, 5), T["d", k]
-            stt(V[:], d[:], 0.0, T["D", k][:], ALU.is_gt, ALU.mult)
-            stt(U[:], d[:], 0.0, T["N", k][:], ALU.is_gt, ALU.mult)
-            tt(V[:], T["fn", k][:], V[:], ALU.subtract)
-            tt(U[:], T["fc", k][:], U[:], ALU.subtract)
-            stt(T["jn", k][:], T["jn", k][:], 1.0, T["i", k][:], ALU.subtract, ALU.mult)
+        def finish_v(k, engine):
+            engine.tensor_tensor(out=T["V", k][:], in0=T["fn", k][:], in1=T["V", k][:], op=ALU.subtract)
+
+        def stage_a(k, after_d=None, before_u=None):
+            fn, fc, iz = new("fn", k, 2), X[(k + 1) % 2], new("iz", k, 1)
+            D, N, U, V, M2 = (new(name, k, 5) for name in ("D", "N", "U", "V", "M2"))
+            fP, iP, rpP = T["fP", k], T["iP", k], T["rpP", k]
+            ahead = k < 4
+            if 1 <= k <= 4:
+                pre_t(k + 2, pool)
+            tt(fc[:], fP[:], T["c", k][:], ALU.mult)
+            tt(iz[:], iP[:], T["z", k][:], ALU.mult)
+            pool.tensor_tensor(out=N[:], in0=fc[:], in1=iz[:], op=ALU.add)
+            if k in (0, 5):
+                pre_t(k + 2, pool)
+            if k >= 1 and k != 5:
+                finish_v(k - 1, pool)
+            tt(fn[:], fP[:], T["n", k][:], ALU.mult)
+            if ahead:
+                s1_gates(k + 1)
+                pre_d(k + 2)
+                move("f", k + 1)
+            stt(T["jn", k][:], T["jn", k][:], 1.0, iP[:], ALU.subtract, ALU.mult)
+            tt(D[:], iP[:], fn[:], ALU.add)
+            if ahead:
+                move("i", k + 1)
+                s1_cell(k + 1)
+            if after_d is not None:
+                after_d()
+            stt(U[:], rpP[:], 0.0, N[:], ALU.is_gt, ALU.mult)
+            stt(sorted_cols(M2), natural_cols(rpP[:]), 0.0, natural_cols(T["gm", k][:]), ALU.is_gt, ALU.mult)
+            stt(V[:], rpP[:], 0.0, D[:], ALU.is_gt, ALU.mult)
+            if ahead:
+                move("rp", k + 1)
+            if before_u is not None:
+                before_u()
+            tt(U[:], fc[:], U[:], ALU.subtract)
 
         def s_abs(k):
             act.activation(out=new("r2", k, 5)[:], in_=T["D", k][:], func=ACT.Abs, bias=EPS)
@@ -131,14 +163,19 @@ def tile_slstmcell_v_kernel(tc, x, h, c, n, m, W_i, b_i, W_f, b_f, W_o, b_o, W_z
         def s_ln(k):
             act.activation(out=T["r2", k][:], in_=T["r2", k][:], func=ACT.Ln)
 
-        def s2(k):
+        def s_exp(k):
             act.activation(out=T["r2", k][:], in_=T["r2", k][:], func=ACT.Exp, scale=-2.0)
-            act.activation(out=new("th", k, 2)[:], in_=T["ot", k][:], func=ACT.Tanh, scale=0.5)
-            act.activation(out=sorted_cols(new("gmn", k, 2)), in_=natural_cols(T["grad", k][:, 3, :]),
+
+        def s2(k):
+            act.activation(out=new("th", k, 3)[:], in_=T["ot", k][:], func=ACT.Tanh, scale=0.5)
+            act.activation(out=sorted_cols(new("gmn", k, 2)), in_=natural_cols(T["gm", k][:]),
                            func=ACT.Copy, scale=-1.0)
 
         def v_go(k):
             stt(new("g2", k, 1)[:], T["th", k][:], 1.0, T["grad", k][:, 0, :], ALU.add, ALU.mult)
+
+        def v_g2(k):
+            stt(T["g2", k][:], T["g2", k][:], 0.5, T["r2", k][:], ALU.mult, ALU.mult)
 
         def add_blocks(key, tile, start=False, stop=False):
             for t in range(PACK):
@@ -148,32 +185,37 @@ def tile_slstmcell_v_kernel(tc, x, h, c, n, m, W_i, b_i, W_f, b_f, W_o, b_o, W_z
 
         def b_first(k):
             g2, grad, D, N = T["g2", k], T["grad", k], T["D", k], T["N", k]
-            G, H, dn, M2 = new("G", k, 1), new("H", k, 1), new("dn", k, 1), new("M2", k, 2)
-            stt(g2[:], g2[:], 0.5, T["r2", k][:], ALU.mult, ALU.mult)
-            stt(sorted_cols(M2), natural_cols(T["d", k][:]), 0.0, natural_cols(grad[:, 3, :]), ALU.is_gt, ALU.mult)
+            G, H, dn = new("G", k, 3), new("H", k, 3), new("dn", k, 1)
             stt(G[:], D[:], EPS, g2[:], ALU.add, ALU.mult)
             stt(dn[:], g2[:], -1.0, N[:], ALU.mult, ALU.mult)
             stt(H[:], G[:], -0.5, N[:], ALU.mult, ALU.mult)
             tt(dn[:], dn[:], grad[:, 2, :], ALU.add)
             tt(G[:], G[:], grad[:, 1, :], ALU.add)
 
-        def b_second(k):
-            dc, dn = T["G", k], T["dn", k]
-            t1, t2 = new("t1", k, 2), new("t2", k, 2)
-            doz = new("doz", k, 2, shape=(P, 2, DIM), dtype=BF16)
+        def open_sums(k):
             bank("sum_f", ("sum_f", k))
             bank("sum_i", ("sum_i", k))
             add_blocks(("sum_f", k), T["M2", k], start=True)
             add_blocks(("sum_i", k), T["gmn", k], start=True)
             add_blocks(("sum_i", k), T["M2", k])
+
+        def b_second(k):
+            dc, dn = T["G", k], T["dn", k]
+            t1, t2 = new("t1", k, 1), new("t2", k, 1)
             tt(sorted_cols(t2), natural_cols(dn[:]), natural_cols(T["V", k][:]), ALU.mult)
             add_blocks(("sum_f", k), t2)
             add_blocks(("sum_i", k), t2)
             tt(sorted_cols(t1), natural_cols(dc[:]), natural_cols(T["U", k][:]), ALU.mult)
             add_blocks(("sum_f", k), t1, stop=True)
             add_blocks(("sum_i", k), t1, stop=True)
+
+        def v_do(k):
+            doz = new("doz", k, 2, shape=(P, 2, DIM), dtype=BF16)
             stt(doz[:, 0, :], T["th", k][:], 1.0, T["H", k][:], ALU.subtract, ALU.mult)
-            stt(doz[:, 1, :], dc[:], -1.0, T["jn", k][:], ALU.mult, ALU.mult)
+
+        def v_dz(k):
+            doz = T["doz", k]
+            stt(doz[:, 1, :], T["G", k][:], -1.0, T["jn", k][:], ALU.mult, ALU.mult)
             oz = bank("oz", ("oz", k), shape=(P, 2, 2, P))
             for g in range(2):
                 words = doz[:, g, :].bitcast(F32)
@@ -181,13 +223,15 @@ def tile_slstmcell_v_kernel(tc, x, h, c, n, m, W_i, b_i, W_f, b_f, W_o, b_o, W_z
                     pe.transpose(oz[:, g, u, :], words[:, u:2 * P:2], ident[:])
 
         def copy_f(k):
-            dT = new("dT", k, 2, shape=(P, 4, DIM), dtype=BF16)
+            dT = new("dT", k, 4, shape=(P, 4, DIM), dtype=BF16)
             act.copy(out=dT[:, 1, :].rearrange("p (r t) -> p r t", t=PACK),
                      in_=T["sum_f", k][:].rearrange("p (t r) -> p r t", t=PACK))
-            words = dT[:, 1, :].bitcast(F32)
+
+        def back(k):
+            words = T["dT", k][:, 1, :].bitcast(F32)
             for u in range(2):
                 if k % PACK == 0:
-                    bank("back%d" % u, ("back", k // PACK, u), shape=(P, PACK, P))
+                    bank((("d", "fP"), ("iP", "rpP"))[k // PACK][u], ("back", k // PACK, u), shape=(P, PACK, P))
                 pe.transpose(T["back", k // PACK, u][:, k % PACK, :], words[:, u:2 * P:2], ident[:])
 
         def copy_i(k):
@@ -217,7 +261,7 @@ def tile_slstmcell_v_kernel(tc, x, h, c, n, m, W_i, b_i, W_f, b_f, W_o, b_o, W_z
                              start=g == 0, stop=g == 3)
 
         def store_0(k):
-            res = new("res", ("o0", k), 3)
+            res = new("res", ("o0", k), 2)
             act.copy(out=res[:], in_=T["acc0", k][:])
             dma.dma_start(out=rows(out_0, k), in_=res[:])
 
@@ -244,10 +288,13 @@ def tile_slstmcell_v_kernel(tc, x, h, c, n, m, W_i, b_i, W_f, b_f, W_o, b_o, W_z
                          start=g == 0, stop=g == 1)
 
         def store_1(t, half, copy):
-            res = new("res", ("o1", t, half), 3)
+            res = new(("D", "N")[half], ("o1", t), 5)
             copy(out=res[:], in_=T["acc1", t, half][:])
             dma.dma_start(out=out_1_rows[t][:, half * DIM:(half + 1) * DIM], in_=res[:])
 
+        load_d(0)
+        load_d(1)
+        load_raw(0)
         load_a(0)
         load_a(1)
         warm = new("warm", 0, 1, shape=(P, 1))
@@ -255,122 +302,173 @@ def tile_slstmcell_v_kernel(tc, x, h, c, n, m, W_i, b_i, W_f, b_f, W_o, b_o, W_z
         act.activation(out=warm[:], in_=warm[:], func=ACT.Exp)
         ident = new("ident", 0, 1, shape=(P, P))
         make_identity(nc, ident[:])
-        load_raw(0)
-        pre_t(0)
+        X = [new("X", e, 2) for e in range(2)]
+        pre_t(0, vec)
         pre_d(0)
-        s1(0)
-        load_a(2)
-        pre_t(1)
+        s1_gates(0)
+        s1_cell(0)
+        load_d(2)
+        load_raw(1)
+        pre_t(1, vec)
+        interleave(0, vec.tensor_copy)
+        move("f", 0)
+        move("i", 0)
         pre_d(1)
-        s1(1)
+        move("rp", 0)
+
+        def ln_first():
+            s2(0)
+            s_ln(0)
+            s_ln(1)
+            s_ln(2)
+            s_abs(3)
+            s_ln(3)
+            s_exp(0)
 
         for k in range(5):
-            if k >= 1:
-                load_a(k + 2)
-            if k < 3:
-                load_raw(k + 1)
+            load_d(k + 3)
+            load_a(k + 2)
+            if k == 2:
+                load_raw(2)
             if k >= 2:
                 load_b(k - 2)
-            a_first(k, ahead=k >= 1)
-            if k == 4:
-                s2(0)
-            if k >= 1:
-                s1(k + 1)
             if k == 3:
-                s_ln(0)
-                s_ln(1)
-                s_ln(2)
-            s_abs(k)
-            if k == 3:
-                s_ln(3)
-            if 1 <= k <= 3:
-                quantize_raw(k - 1)
-            a_second(k)
-            if k < 3:
-                interleave(k)
-        v_go(0)
+                stage_a(k, ln_first)
+            elif k == 2:
+                stage_a(k, lambda: s_abs(k), lambda: quantize_raw(1))
+            elif k == 4:
+                stage_a(k, lambda: s_abs(k), lambda: v_go(0))
+            elif k == 0:
+                stage_a(k, lambda: s_abs(k), lambda: quantize_raw(0))
+            else:
+                stage_a(k, lambda: s_abs(k))
+            if k < 2:
+                interleave(1, act.copy, k)
+        v_g2(0)
+        finish_v(4, vec)
 
+        late = 7
+        raw_at = {0: 2, 1: 3, 2: 4, 3: 5, 5: 6, 6: 7}
         for k in range(CHUNKS):
+            last = k == CHUNKS - 1
+            if k == 1:
+                load_a(7)
             if 1 <= k <= 5:
                 load_b(k + 2)
-            if k <= 3:
-                load_raw(k + 4)
-            if k + 1 < CHUNKS:
+            if k + 1 in raw_at:
+                load_raw(raw_at[k + 1])
+            if k < 3:
+                s1_gates(k + 5)
+            if not last:
+                s_exp(k + 1)
                 s2(k + 1)
-            b_first(k)
-            if 1 <= k <= 3:
-                store_0(k - 1)
             if k >= 4:
-                copies(k - 1)
-            if k >= 5:
+                copy_f(k - 1)
+                copy_i(k - 1)
+                if k - 1 < late:
+                    copy_oz(k - 1)
+                back(k - 1)
+            if k == 3:
+                for e in range(3):
+                    back(e)
+            open_sums(k)
+            if k < 3:
+                if k < 2:
+                    pre_d(k + 6)
+                move("f", k + 5)
+                move("i", k + 5)
+                move("rp", k + 5)
+                s1_cell(k + 5)
+            b_first(k)
+            if k in (2, 3):
                 store_0(k - 2)
             if k == 4:
                 back_copy(0, 0, act.copy)
                 back_copy(0, 1, act.copy)
-            s = {0: 3, 1: 4, 2: 5, 3: 6, 5: 7}.get(k)
+            s = raw_at.get(k)
             if s is not None:
-                interleave(s)
-            b_second(k)
-            if k + 1 < CHUNKS:
-                v_go(k + 1)
-            if k >= 4:
+                interleave(s, act.copy)
+            if last:
+                store_0(k - 2)
                 product_0(k - 1)
+            b_second(k)
+            if last:
+                break
+            v_go(k + 1)
+            if k < late:
+                v_do(k)
             if k == 5:
                 quantize_back(0, 0)
+            v_g2(k + 1)
+            if k < late:
+                v_dz(k)
+            if k == 5:
                 quantize_back(0, 1)
-            if s is not None:
+            if 3 <= k and k - 1 < late:
+                if k > 3:
+                    store_0(k - 2)
+                product_0(k - 1)
+            if s is not None and k >= 3:
                 quantize_raw(s)
             if k == 6:
-                pass_1(2, 0, 0, "acc1a")
-                pass_1(2, 1, 0, "acc1b")
+                pass_1(2, 0, 0, "d")
+                pass_1(2, 1, 0, "fP")
             if k < 3:
                 a = k + 5
-                if a == 5:
-                    load_a(7)
-                a_first(a, ahead=a < 7)
-                if a < 7:
-                    s1(a + 1)
-                    copies(k)
-                    s_abs(a)
-                else:
-                    s_ln(4)
-                    s_ln(5)
-                    copies(k)
-                    s_ln(6)
-                    s_abs(7)
-                    s_ln(7)
-                a_second(a)
-                product_0(k)
+
+                def after_d():
+                    if a < 7:
+                        copies(k)
+                        s_abs(a)
+                    else:
+                        s_ln(4)
+                        copies(k)
+                        s_ln(5)
+                        s_ln(6)
+                        s_abs(7)
+                        s_ln(7)
+
+                def before_u():
+                    quantize_raw(s)
+                    if k > 0:
+                        product_0(k - 1)
+
+                stage_a(a, after_d, before_u)
+                if a == 7:
+                    finish_v(7, vec)
 
         last = CHUNKS - 1
         copy_f(last)
+        back(last)
         copy_i(last)
+        v_do(last)
+        v_dz(last)
+        back_copy(1, 1, act.copy)
+        back_copy(1, 0, vec.tensor_copy)
         pass_1(3, 0, 0, "sum_f")
         pass_1(3, 1, 0, "sum_i")
-        back_copy(1, 1, vec.tensor_copy)
-        back_copy(1, 0, act.copy)
         copy_oz(last)
         store_0(last - 1)
-        pass_1(0, 0, 0, "oz")
-        pass_1(0, 1, 0, "back1")
         quantize_back(1, 1)
-        pass_1(1, 0, 0, "back0")
+        pass_1(0, 0, 0, "oz")
         quantize_back(1, 0)
         pass_1(2, 0, 1)
         pass_1(2, 1, 1)
-        product_0(last)
         pass_1(3, 0, 1)
         pass_1(3, 1, 1)
+        product_0(last)
         pass_1(0, 0, 1)
-        pass_1(0, 1, 1)
-        pass_1(1, 0, 1)
         store_1(2, 0, act.copy)
-        pass_1(1, 1, 0, "acc1a")
-        pass_1(1, 1, 1)
         store_1(2, 1, vec.tensor_copy)
+        pass_1(0, 1, 0, "iP")
+        pass_1(0, 1, 1)
+        pass_1(1, 0, 0, "rpP")
+        pass_1(1, 0, 1)
+        pass_1(1, 1, 0, "d")
+        pass_1(1, 1, 1)
+        store_1(3, 0, act.copy)
+        store_1(3, 1, vec.tensor_copy)
         store_0(last)
-        store_1(3, 0, vec.tensor_copy)
-        store_1(3, 1, act.copy)
         store_1(0, 0, vec.tensor_copy)
         store_1(0, 1, act.copy)
         store_1(1, 0, vec.tensor_copy)

@@ -63,8 +63,9 @@ def tile_slstmcell_v_kernel(tc, x, h, c, n, m, W_i, b_i, W_f, b_f, W_o, b_o, W_z
             return ap.rearrange("p (q t) -> p q t", t=PACK)
 
         def load_d(k):
-            dma.dma_start(out=new("gif", k, 2, shape=(P, 2 * DIM))[:], in_=rows(gates, k)[:, 0:2 * DIM])
+            dma.dma_start(out=new("gi", k, 2)[:], in_=rows(gates, k)[:, 0:DIM])
             dma.dma_start(out=new("m", k, 2, dtype=BF16)[:], in_=rows(m, k))
+            dma.dma_start(out=new("gf", k, 2)[:], in_=rows(gates, k)[:, DIM:2 * DIM])
 
         def load_a(k):
             dma.dma_start(out=new("c", k, 3, dtype=BF16)[:], in_=rows(c, k))
@@ -95,19 +96,18 @@ def tile_slstmcell_v_kernel(tc, x, h, c, n, m, W_i, b_i, W_f, b_f, W_o, b_o, W_z
                             in_=T["grouped", s][:].rearrange("p w j -> p (w j)"))
 
         def pre_t(k, engine):
-            T["t", k] = new("H", "t", 3) if k == 1 else X[k % 2]
-            engine.tensor_tensor(out=T["t", k][:], in0=T["m", k][:], in1=T["gif", k][:, 0:DIM], op=ALU.subtract)
+            T["t", k] = new("H", "t", 1) if k == 1 else X[k % 2]
+            engine.tensor_tensor(out=T["t", k][:], in0=T["m", k][:], in1=T["gi", k][:], op=ALU.subtract)
 
         def pre_d(k):
             bank("d", ("d", k))
-            add_blocks(("d", k), T["gif", k][:, DIM:2 * DIM], start=True)
+            add_blocks(("d", k), T["gf", k], start=True)
             add_blocks(("d", k), T["t", k], stop=True)
 
         def s1_gates(k):
             i, f, rp, d = new("i", k, 1), new("f", k, 1), new("rp", k, 1), T["d", k]
-            act.activation(out=f[:], in_=d[:], func=ACT.Relu, scale=-1.0)
             act.activation(out=rp[:], in_=d[:], func=ACT.Relu)
-            act.activation(out=f[:], in_=f[:], func=ACT.Exp, scale=-1.0)
+            act.activation(out=f[:], in_=d[:], func=ACT.Exp)
             act.activation(out=i[:], in_=rp[:], func=ACT.Exp, scale=-1.0)
 
         def s1_cell(k):
@@ -120,7 +120,13 @@ def tile_slstmcell_v_kernel(tc, x, h, c, n, m, W_i, b_i, W_f, b_f, W_o, b_o, W_z
             add_blocks((name + "P", k), T[name, k], start=True, stop=True)
 
         def finish_v(k, engine):
-            engine.tensor_tensor(out=T["V", k][:], in0=T["fn", k][:], in1=T["V", k][:], op=ALU.subtract)
+            masked = T["V", k]
+            if 4 <= k <= 6:
+                T["V", k] = Y[k - 4]
+            engine.tensor_tensor(out=T["V", k][:], in0=T["fn", k][:], in1=masked[:], op=ALU.subtract)
+
+        def finish_u(k, engine):
+            engine.tensor_tensor(out=T["U", k][:], in0=X[(k + 1) % 2][:], in1=T["U", k][:], op=ALU.subtract)
 
         def stage_a(k, after_d=None, before_u=None):
             fn, fc, iz = new("fn", k, 2), X[(k + 1) % 2], new("iz", k, 1)
@@ -129,14 +135,18 @@ def tile_slstmcell_v_kernel(tc, x, h, c, n, m, W_i, b_i, W_f, b_f, W_o, b_o, W_z
             ahead = k < 4
             if 1 <= k <= 4:
                 pre_t(k + 2, pool)
-            tt(fc[:], fP[:], T["c", k][:], ALU.mult)
+            if k >= 5:
+                finish_v(k - 1, pool)
+            stt(fc[:], fP[:], 1.0, T["c", k][:], ALU.min, ALU.mult)
             tt(iz[:], iP[:], T["z", k][:], ALU.mult)
             pool.tensor_tensor(out=N[:], in0=fc[:], in1=iz[:], op=ALU.add)
             if k in (0, 5):
                 pre_t(k + 2, pool)
-            if k >= 1 and k != 5:
+            if 1 <= k <= 4:
                 finish_v(k - 1, pool)
-            tt(fn[:], fP[:], T["n", k][:], ALU.mult)
+            if k >= 6:
+                finish_u(k - 1, pool)
+            stt(fn[:], fP[:], 1.0, T["n", k][:], ALU.min, ALU.mult)
             if ahead:
                 s1_gates(k + 1)
                 pre_d(k + 2)
@@ -148,14 +158,15 @@ def tile_slstmcell_v_kernel(tc, x, h, c, n, m, W_i, b_i, W_f, b_f, W_o, b_o, W_z
                 s1_cell(k + 1)
             if after_d is not None:
                 after_d()
-            stt(U[:], rpP[:], 0.0, N[:], ALU.is_gt, ALU.mult)
             stt(sorted_cols(M2), natural_cols(rpP[:]), 0.0, natural_cols(T["gm", k][:]), ALU.is_gt, ALU.mult)
+            stt(U[:], rpP[:], 0.0, N[:], ALU.is_gt, ALU.mult)
             stt(V[:], rpP[:], 0.0, D[:], ALU.is_gt, ALU.mult)
             if ahead:
                 move("rp", k + 1)
             if before_u is not None:
                 before_u()
-            tt(U[:], fc[:], U[:], ALU.subtract)
+            if k not in (5, 6):
+                finish_u(k, vec)
 
         def s_abs(k):
             act.activation(out=new("r2", k, 5)[:], in_=T["D", k][:], func=ACT.Abs, bias=EPS)
@@ -167,7 +178,7 @@ def tile_slstmcell_v_kernel(tc, x, h, c, n, m, W_i, b_i, W_f, b_f, W_o, b_o, W_z
             act.activation(out=T["r2", k][:], in_=T["r2", k][:], func=ACT.Exp, scale=-2.0)
 
         def s2(k):
-            act.activation(out=new("th", k, 3)[:], in_=T["ot", k][:], func=ACT.Tanh, scale=0.5)
+            act.activation(out=new("th", k, 2)[:], in_=T["ot", k][:], func=ACT.Tanh, scale=0.5)
             act.activation(out=sorted_cols(new("gmn", k, 2)), in_=natural_cols(T["gm", k][:]),
                            func=ACT.Copy, scale=-1.0)
 
@@ -183,12 +194,16 @@ def tile_slstmcell_v_kernel(tc, x, h, c, n, m, W_i, b_i, W_f, b_f, W_o, b_o, W_z
                 pe.matmul(T[key][:, cols], lhsT=tile[:, cols], rhs=ident[:], is_transpose=True,
                           start=start and t == 0, stop=stop and t == PACK - 1)
 
-        def b_first(k):
+        def b_first(k, last):
             g2, grad, D, N = T["g2", k], T["grad", k], T["D", k], T["N", k]
-            G, H, dn = new("G", k, 3), new("H", k, 3), new("dn", k, 1)
+            G, H, dn = Y[min(k, 3)], new("H", k, 1), new("dn", k, 1)
+            T["G", k] = G
             stt(G[:], D[:], EPS, g2[:], ALU.add, ALU.mult)
             stt(dn[:], g2[:], -1.0, N[:], ALU.mult, ALU.mult)
             stt(H[:], G[:], -0.5, N[:], ALU.mult, ALU.mult)
+            if last:
+                store_0(k - 2)
+                product_0(k - 1)
             tt(dn[:], dn[:], grad[:, 2, :], ALU.add)
             tt(G[:], G[:], grad[:, 1, :], ALU.add)
 
@@ -303,6 +318,7 @@ def tile_slstmcell_v_kernel(tc, x, h, c, n, m, W_i, b_i, W_f, b_f, W_o, b_o, W_z
         ident = new("ident", 0, 1, shape=(P, P))
         make_identity(nc, ident[:])
         X = [new("X", e, 2) for e in range(2)]
+        Y = [new("Y", e, 4) for e in range(4)]
         pre_t(0, vec)
         pre_d(0)
         s1_gates(0)
@@ -317,7 +333,6 @@ def tile_slstmcell_v_kernel(tc, x, h, c, n, m, W_i, b_i, W_f, b_f, W_o, b_o, W_z
         move("rp", 0)
 
         def ln_first():
-            s2(0)
             s_ln(0)
             s_ln(1)
             s_ln(2)
@@ -330,12 +345,13 @@ def tile_slstmcell_v_kernel(tc, x, h, c, n, m, W_i, b_i, W_f, b_f, W_o, b_o, W_z
             load_a(k + 2)
             if k == 2:
                 load_raw(2)
-            if k >= 2:
-                load_b(k - 2)
+            if k in (1, 3, 4):
+                load_b(max(k - 2, 0))
             if k == 3:
                 stage_a(k, ln_first)
             elif k == 2:
-                stage_a(k, lambda: s_abs(k), lambda: quantize_raw(1))
+                stage_a(k, lambda: s_abs(k))
+                s2(0)
             elif k == 4:
                 stage_a(k, lambda: s_abs(k), lambda: v_go(0))
             elif k == 0:
@@ -345,7 +361,7 @@ def tile_slstmcell_v_kernel(tc, x, h, c, n, m, W_i, b_i, W_f, b_f, W_o, b_o, W_z
             if k < 2:
                 interleave(1, act.copy, k)
         v_g2(0)
-        finish_v(4, vec)
+        quantize_raw(1)
 
         late = 7
         raw_at = {0: 2, 1: 3, 2: 4, 3: 5, 5: 6, 6: 7}
@@ -372,6 +388,9 @@ def tile_slstmcell_v_kernel(tc, x, h, c, n, m, W_i, b_i, W_f, b_f, W_o, b_o, W_z
                 for e in range(3):
                     back(e)
             open_sums(k)
+            if k == 6:
+                pass_1(2, 0, 0, "d")
+                pass_1(2, 1, 0, "fP")
             if k < 3:
                 if k < 2:
                     pre_d(k + 6)
@@ -379,7 +398,7 @@ def tile_slstmcell_v_kernel(tc, x, h, c, n, m, W_i, b_i, W_f, b_f, W_o, b_o, W_z
                 move("i", k + 5)
                 move("rp", k + 5)
                 s1_cell(k + 5)
-            b_first(k)
+            b_first(k, last)
             if k in (2, 3):
                 store_0(k - 2)
             if k == 4:
@@ -388,9 +407,6 @@ def tile_slstmcell_v_kernel(tc, x, h, c, n, m, W_i, b_i, W_f, b_f, W_o, b_o, W_z
             s = raw_at.get(k)
             if s is not None:
                 interleave(s, act.copy)
-            if last:
-                store_0(k - 2)
-                product_0(k - 1)
             b_second(k)
             if last:
                 break
@@ -410,9 +426,6 @@ def tile_slstmcell_v_kernel(tc, x, h, c, n, m, W_i, b_i, W_f, b_f, W_o, b_o, W_z
                 product_0(k - 1)
             if s is not None and k >= 3:
                 quantize_raw(s)
-            if k == 6:
-                pass_1(2, 0, 0, "d")
-                pass_1(2, 1, 0, "fP")
             if k < 3:
                 a = k + 5
 
@@ -437,39 +450,38 @@ def tile_slstmcell_v_kernel(tc, x, h, c, n, m, W_i, b_i, W_f, b_f, W_o, b_o, W_z
                 if a == 7:
                     finish_v(7, vec)
 
-        last = CHUNKS - 1
-        copy_f(last)
-        back(last)
-        copy_i(last)
-        v_do(last)
-        v_dz(last)
-        back_copy(1, 1, act.copy)
-        back_copy(1, 0, vec.tensor_copy)
+        copy_f(7)
+        back(7)
+        copy_i(7)
+        v_do(7)
+        v_dz(7)
         pass_1(3, 0, 0, "sum_f")
         pass_1(3, 1, 0, "sum_i")
-        copy_oz(last)
-        store_0(last - 1)
+        back_copy(1, 1, vec.tensor_copy)
+        back_copy(1, 0, act.copy)
+        store_0(6)
+        copy_oz(7)
         quantize_back(1, 1)
-        pass_1(0, 0, 0, "oz")
-        quantize_back(1, 0)
         pass_1(2, 0, 1)
         pass_1(2, 1, 1)
         pass_1(3, 0, 1)
         pass_1(3, 1, 1)
-        product_0(last)
+        quantize_back(1, 0)
+        pass_1(0, 0, 0, "rpP")
         pass_1(0, 0, 1)
-        store_1(2, 0, act.copy)
-        store_1(2, 1, vec.tensor_copy)
         pass_1(0, 1, 0, "iP")
         pass_1(0, 1, 1)
-        pass_1(1, 0, 0, "rpP")
-        pass_1(1, 0, 1)
-        pass_1(1, 1, 0, "d")
-        pass_1(1, 1, 1)
+        store_1(2, 0, act.copy)
+        store_1(2, 1, vec.tensor_copy)
+        product_0(7)
         store_1(3, 0, act.copy)
+        pass_1(1, 0, 0, "d")
+        pass_1(1, 0, 1)
+        pass_1(1, 1, 0, "fP")
+        pass_1(1, 1, 1)
         store_1(3, 1, vec.tensor_copy)
-        store_0(last)
-        store_1(0, 0, vec.tensor_copy)
-        store_1(0, 1, act.copy)
+        store_1(0, 0, act.copy)
+        store_1(0, 1, vec.tensor_copy)
+        store_0(7)
         store_1(1, 0, vec.tensor_copy)
         store_1(1, 1, act.copy)

from contextlib import ExitStack

import concourse.mybir as mybir
from concourse.masks import make_identity

B, DIM = 1024, 512
FLOPS = 2 * B * 4 * DIM * DIM + 2 * B * DIM * 2 * DIM
BYTES = B * 4 * DIM * 4 + 4 * B * DIM * 2 + 5 * B * DIM * 2 + 4 * DIM * DIM * 2 + 2 * B * DIM * 4

F32 = mybir.dt.float32
BF16 = mybir.dt.bfloat16
U32 = mybir.dt.uint32
U8 = mybir.dt.uint8
E4M3 = mybir.dt.float8_e4m3fn_x4
E5M2 = mybir.dt.float8_e5m2_x4
ALU = mybir.AluOpType
ACT = mybir.ActivationFunctionType

P = 128
PACK = 4
CHUNKS = 8
EPS = 1e-6


def tile_slstmcell_v_kernel(tc, x, h, c, n, m, W_i, b_i, W_f, b_f, W_o, b_o, W_z, b_z,
                                        gates, grad_out, out_0, out_1):
    nc = tc.nc
    vec, act, pe, pool, dma = nc.vector, nc.scalar, nc.tensor, nc.gpsimd, nc.sync

    def rows(ap, k):
        return ap.rearrange("(g p j) w -> g j p w", g=2, j=PACK)[k // PACK, k % PACK]

    grad_rows = grad_out.rearrange("s (g p j) w -> g j p s w", g=2, j=PACK)
    out_1_rows = out_1.rearrange("(p t) w -> t p w", t=PACK)
    sources = [w[:, 0:DIM] for w in (W_i, W_f, W_o, W_z)]
    sources = sources + [x[0:512, :], h[0:512, :], x[512:1024, :], h[512:1024, :]]

    with ExitStack() as ctx:
        sb = ctx.enter_context(tc.tile_pool(name="sb", bufs=1))
        ps = ctx.enter_context(tc.psum_pool(name="ps", bufs=1))
        ctx.enter_context(tc.manual_schedule())

        T = {}

        def new(name, k, bufs, shape=(P, DIM), dtype=F32):
            T[name, k] = sb.tile(list(shape), dtype, name=name, tag=name, bufs=bufs, align_bytes=64)
            return T[name, k]

        def bank(tag, key, shape=(P, DIM)):
            T[key] = ps.tile(list(shape), F32, name=tag, tag=tag)
            return T[key]

        def tt(out, in0, in1, op):
            vec.tensor_tensor(out=out, in0=in0, in1=in1, op=op)

        def stt(out, in0, scalar, in1, op0, op1):
            vec.scalar_tensor_tensor(out=out, in0=in0, scalar=scalar, in1=in1, op0=op0, op1=op1)

        def sorted_cols(tile):
            return tile[:].rearrange("p (t q) -> p q t", t=PACK)

        def natural_cols(ap):
            return ap.rearrange("p (q t) -> p q t", t=PACK)

        def load_d(k):
            dma.dma_start(out=new("gi", k, 2)[:], in_=rows(gates, k)[:, 0:DIM])
            dma.dma_start(out=new("m", k, 2, dtype=BF16)[:], in_=rows(m, k))
            dma.dma_start(out=new("gf", k, 2)[:], in_=rows(gates, k)[:, DIM:2 * DIM])

        def load_a(k):
            dma.dma_start(out=new("c", k, 3, dtype=BF16)[:], in_=rows(c, k))
            dma.dma_start(out=new("gz", k, 2)[:], in_=rows(gates, k)[:, 3 * DIM:4 * DIM])
            dma.dma_start(out=new("n", k, 3, dtype=BF16)[:], in_=rows(n, k))
            dma.dma_start(out=new("gm", k, 8, dtype=BF16)[:], in_=grad_rows[k // PACK, k % PACK][:, 3, :])

        def load_b(k):
            dma.dma_start(out=new("ot", k, 3)[:], in_=rows(gates, k)[:, 2 * DIM:3 * DIM])
            dma.dma_start(out=new("grad", k, 3, shape=(P, 3, DIM), dtype=BF16)[:],
                          in_=grad_rows[k // PACK, k % PACK][:, 0:3, :])

        def load_raw(s):
            dma.dma_start(out=new("raw", s, 2, shape=(P, PACK, DIM), dtype=BF16)[:],
                          in_=sources[s].rearrange("(p j) w -> p j w", j=PACK))

        def interleave(s, copy, half=None):
            if half != 1:
                new("grouped", s, 1, shape=(P, DIM, PACK), dtype=BF16)
            cols = slice(0, DIM) if half is None else slice(half * DIM // 2, (half + 1) * DIM // 2)
            copy(out=T["grouped", s][:, cols, :].rearrange("p (c i) t -> p c t i", i=4),
                 in_=T["raw", s][:, :, cols].rearrange("p t (c i) -> p c t i", i=4))

        def quantize_raw(s):
            codes = new("e4_codes", s, 8, dtype=U32)
            scales = new("e4_scales", s, 8, dtype=U8)
            vec.quantize_mx(out=codes[:].bitcast(E4M3), scales=scales[:],
                            in_=T["grouped", s][:].rearrange("p w j -> p (w j)"))

        def pre_t(k, engine):
            T["t", k] = new("H", "t", 1) if k == 1 else X[k % 2]
            engine.tensor_tensor(out=T["t", k][:], in0=T["m", k][:], in1=T["gi", k][:], op=ALU.subtract)

        def pre_d(k):
            bank("d", ("d", k))
            add_blocks(("d", k), T["gf", k], start=True)
            add_blocks(("d", k), T["t", k], stop=True)

        def s1_gates(k):
            i, f, rp, d = new("i", k, 1), new("f", k, 1), new("rp", k, 1), T["d", k]
            act.activation(out=rp[:], in_=d[:], func=ACT.Relu)
            act.activation(out=f[:], in_=d[:], func=ACT.Exp)
            act.activation(out=i[:], in_=rp[:], func=ACT.Exp, scale=-1.0)

        def s1_cell(k):
            z, jn = new("z", k, 2), new("jn", k, 6)
            act.activation(out=z[:], in_=T["gz", k][:], func=ACT.Tanh)
            act.activation(out=jn[:], in_=z[:], func=ACT.Square)

        def move(name, k):
            bank(name + "P", (name + "P", k))
            add_blocks((name + "P", k), T[name, k], start=True, stop=True)

        def finish_v(k, engine):
            masked = T["V", k]
            if 4 <= k <= 6:
                T["V", k] = Y[k - 4]
            engine.tensor_tensor(out=T["V", k][:], in0=T["fn", k][:], in1=masked[:], op=ALU.subtract)

        def finish_u(k, engine):
            engine.tensor_tensor(out=T["U", k][:], in0=X[(k + 1) % 2][:], in1=T["U", k][:], op=ALU.subtract)

        def stage_a(k, after_d=None, before_u=None):
            fn, fc, iz = new("fn", k, 2), X[(k + 1) % 2], new("iz", k, 1)
            D, N, U, V, M2 = (new(name, k, 5) for name in ("D", "N", "U", "V", "M2"))
            fP, iP, rpP = T["fP", k], T["iP", k], T["rpP", k]
            ahead = k < 4
            if 1 <= k <= 4:
                pre_t(k + 2, pool)
            if k >= 5:
                finish_v(k - 1, pool)
            stt(fc[:], fP[:], 1.0, T["c", k][:], ALU.min, ALU.mult)
            tt(iz[:], iP[:], T["z", k][:], ALU.mult)
            pool.tensor_tensor(out=N[:], in0=fc[:], in1=iz[:], op=ALU.add)
            if k in (0, 5):
                pre_t(k + 2, pool)
            if 1 <= k <= 4:
                finish_v(k - 1, pool)
            if k >= 6:
                finish_u(k - 1, pool)
            stt(fn[:], fP[:], 1.0, T["n", k][:], ALU.min, ALU.mult)
            if ahead:
                s1_gates(k + 1)
                pre_d(k + 2)
                move("f", k + 1)
            stt(T["jn", k][:], T["jn", k][:], 1.0, iP[:], ALU.subtract, ALU.mult)
            tt(D[:], iP[:], fn[:], ALU.add)
            if ahead:
                move("i", k + 1)
                s1_cell(k + 1)
            if after_d is not None:
                after_d()
            stt(sorted_cols(M2), natural_cols(rpP[:]), 0.0, natural_cols(T["gm", k][:]), ALU.is_gt, ALU.mult)
            stt(U[:], rpP[:], 0.0, N[:], ALU.is_gt, ALU.mult)
            stt(V[:], rpP[:], 0.0, D[:], ALU.is_gt, ALU.mult)
            if ahead:
                move("rp", k + 1)
            if before_u is not None:
                before_u()
            if k not in (5, 6):
                finish_u(k, vec)

        def s_abs(k):
            act.activation(out=new("r2", k, 5)[:], in_=T["D", k][:], func=ACT.Abs, bias=EPS)

        def s_ln(k):
            act.activation(out=T["r2", k][:], in_=T["r2", k][:], func=ACT.Ln)

        def s_exp(k):
            act.activation(out=T["r2", k][:], in_=T["r2", k][:], func=ACT.Exp, scale=-2.0)

        def s2(k):
            act.activation(out=new("th", k, 2)[:], in_=T["ot", k][:], func=ACT.Tanh, scale=0.5)
            act.activation(out=sorted_cols(new("gmn", k, 2)), in_=natural_cols(T["gm", k][:]),
                           func=ACT.Copy, scale=-1.0)

        def v_go(k):
            stt(new("g2", k, 1)[:], T["th", k][:], 1.0, T["grad", k][:, 0, :], ALU.add, ALU.mult)

        def v_g2(k):
            stt(T["g2", k][:], T["g2", k][:], 0.5, T["r2", k][:], ALU.mult, ALU.mult)

        def add_blocks(key, tile, start=False, stop=False):
            for t in range(PACK):
                cols = slice(t * P, (t + 1) * P)
                pe.matmul(T[key][:, cols], lhsT=tile[:, cols], rhs=ident[:], is_transpose=True,
                          start=start and t == 0, stop=stop and t == PACK - 1)

        def b_first(k, last):
            g2, grad, D, N = T["g2", k], T["grad", k], T["D", k], T["N", k]
            G, H, dn = Y[min(k, 3)], new("H", k, 1), new("dn", k, 1)
            T["G", k] = G
            stt(G[:], D[:], EPS, g2[:], ALU.add, ALU.mult)
            stt(dn[:], g2[:], -1.0, N[:], ALU.mult, ALU.mult)
            stt(H[:], G[:], -0.5, N[:], ALU.mult, ALU.mult)
            if last:
                store_0(k - 2)
                product_0(k - 1)
            tt(dn[:], dn[:], grad[:, 2, :], ALU.add)
            tt(G[:], G[:], grad[:, 1, :], ALU.add)

        def open_sums(k):
            bank("sum_f", ("sum_f", k))
            bank("sum_i", ("sum_i", k))
            add_blocks(("sum_f", k), T["M2", k], start=True)
            add_blocks(("sum_i", k), T["gmn", k], start=True)
            add_blocks(("sum_i", k), T["M2", k])

        def b_second(k):
            dc, dn = T["G", k], T["dn", k]
            t1, t2 = new("t1", k, 1), new("t2", k, 1)
            tt(sorted_cols(t2), natural_cols(dn[:]), natural_cols(T["V", k][:]), ALU.mult)
            add_blocks(("sum_f", k), t2)
            add_blocks(("sum_i", k), t2)
            tt(sorted_cols(t1), natural_cols(dc[:]), natural_cols(T["U", k][:]), ALU.mult)
            add_blocks(("sum_f", k), t1, stop=True)
            add_blocks(("sum_i", k), t1, stop=True)

        def v_do(k):
            doz = new("doz", k, 2, shape=(P, 2, DIM), dtype=BF16)
            stt(doz[:, 0, :], T["th", k][:], 1.0, T["H", k][:], ALU.subtract, ALU.mult)

        def v_dz(k):
            doz = T["doz", k]
            stt(doz[:, 1, :], T["G", k][:], -1.0, T["jn", k][:], ALU.mult, ALU.mult)
            oz = bank("oz", ("oz", k), shape=(P, 2, 2, P))
            for g in range(2):
                words = doz[:, g, :].bitcast(F32)
                for u in range(2):
                    pe.transpose(oz[:, g, u, :], words[:, u:2 * P:2], ident[:])

        def copy_f(k):
            dT = new("dT", k, 4, shape=(P, 4, DIM), dtype=BF16)
            act.copy(out=dT[:, 1, :].rearrange("p (r t) -> p r t", t=PACK),
                     in_=T["sum_f", k][:].rearrange("p (t r) -> p r t", t=PACK))

        def back(k):
            words = T["dT", k][:, 1, :].bitcast(F32)
            for u in range(2):
                if k % PACK == 0:
                    bank((("d", "fP"), ("iP", "rpP"))[k // PACK][u], ("back", k // PACK, u), shape=(P, PACK, P))
                pe.transpose(T["back", k // PACK, u][:, k % PACK, :], words[:, u:2 * P:2], ident[:])

        def copy_i(k):
            act.activation(out=T["dT", k][:, 0, :].rearrange("p (r t) -> p r t", t=PACK),
                           in_=T["sum_i", k][:].rearrange("p (t r) -> p r t", t=PACK),
                           func=ACT.Copy, scale=-1.0)

        def copy_oz(k):
            words = T["dT", k][:, 2:4, :].rearrange("p g w -> p (g w)").bitcast(F32)
            act.copy(out=words.rearrange("p (g r u) -> p g r u", g=2, u=2),
                     in_=T["oz", k][:].rearrange("p g u r -> p g r u"))

        def copies(k):
            copy_f(k)
            copy_i(k)
            copy_oz(k)

        def product_0(k):
            codes, scales = new("d_codes", k, 2, dtype=U32), new("d_scales", k, 2, dtype=U8)
            vec.quantize_mx(out=codes[:].bitcast(E5M2), scales=scales[:],
                            in_=T["dT", k][:].rearrange("p g w -> p (g w)"))
            acc = bank("acc0", ("acc0", k))
            for g in range(4):
                cols = slice(g * P, (g + 1) * P)
                pe.matmul_mx(out=acc[:], lhsT=codes[:, cols].bitcast(E5M2), lhsT_scale=scales[:, cols],
                             rhs=T["e4_codes", g][:].bitcast(E4M3), rhs_scale=T["e4_scales", g][:],
                             start=g == 0, stop=g == 3)

        def store_0(k):
            res = new("res", ("o0", k), 2)
            act.copy(out=res[:], in_=T["acc0", k][:])
            dma.dma_start(out=rows(out_0, k), in_=res[:])

        def back_copy(g, u, copy):
            dfa = new("dfa%d" % u, g, 1, shape=(P, 2 * DIM), dtype=BF16)
            halves = T["back", g, u][:].rearrange("r j p -> r (j p)").bitcast(BF16)
            copy(out=dfa[:].rearrange("r (e p j) -> r e p j", e=2, j=PACK),
                 in_=halves.rearrange("r (j p e) -> r e p j", j=PACK, e=2))

        def quantize_back(g, u):
            codes = new("f_codes", (g, u), 4, shape=(P, 2 * P), dtype=U32)
            scales = new("f_scales", (g, u), 4, shape=(P, 2 * P), dtype=U8)
            vec.quantize_mx(out=codes[:].bitcast(E5M2), scales=scales[:], in_=T["dfa%d" % u, g][:])

        def pass_1(t, half, g, tag=None):
            if g == 0:
                bank(tag, ("acc1", t, half))
            cols = slice((t % 2) * P, (t % 2 + 1) * P)
            s = 4 + 2 * g + half
            pe.matmul_mx(out=T["acc1", t, half][:],
                         lhsT=T["f_codes", (g, t // 2)][:, cols].bitcast(E5M2),
                         lhsT_scale=T["f_scales", (g, t // 2)][:, cols],
                         rhs=T["e4_codes", s][:].bitcast(E4M3), rhs_scale=T["e4_scales", s][:],
                         start=g == 0, stop=g == 1)

        def store_1(t, half, copy):
            res = new(("D", "N")[half], ("o1", t), 5)
            copy(out=res[:], in_=T["acc1", t, half][:])
            dma.dma_start(out=out_1_rows[t][:, half * DIM:(half + 1) * DIM], in_=res[:])

        load_d(0)
        load_d(1)
        load_raw(0)
        load_a(0)
        load_a(1)
        warm = new("warm", 0, 1, shape=(P, 1))
        vec.memset(warm[:], 0.0)
        act.activation(out=warm[:], in_=warm[:], func=ACT.Exp)
        ident = new("ident", 0, 1, shape=(P, P))
        make_identity(nc, ident[:])
        X = [new("X", e, 2) for e in range(2)]
        Y = [new("Y", e, 4) for e in range(4)]
        pre_t(0, vec)
        pre_d(0)
        s1_gates(0)
        s1_cell(0)
        load_d(2)
        load_raw(1)
        pre_t(1, vec)
        interleave(0, vec.tensor_copy)
        move("f", 0)
        move("i", 0)
        pre_d(1)
        move("rp", 0)

        def ln_first():
            s_ln(0)
            s_ln(1)
            s_ln(2)
            s_abs(3)
            s_ln(3)
            s_exp(0)

        for k in range(5):
            load_d(k + 3)
            load_a(k + 2)
            if k == 2:
                load_raw(2)
            if k in (1, 3, 4):
                load_b(max(k - 2, 0))
            if k == 3:
                stage_a(k, ln_first)
            elif k == 2:
                stage_a(k, lambda: s_abs(k))
                s2(0)
            elif k == 4:
                stage_a(k, lambda: s_abs(k), lambda: v_go(0))
            elif k == 0:
                stage_a(k, lambda: s_abs(k), lambda: quantize_raw(0))
            else:
                stage_a(k, lambda: s_abs(k))
            if k < 2:
                interleave(1, act.copy, k)
        v_g2(0)
        quantize_raw(1)

        late = 7
        raw_at = {0: 2, 1: 3, 2: 4, 3: 5, 5: 6, 6: 7}
        for k in range(CHUNKS):
            last = k == CHUNKS - 1
            if k == 1:
                load_a(7)
            if 1 <= k <= 5:
                load_b(k + 2)
            if k + 1 in raw_at:
                load_raw(raw_at[k + 1])
            if k < 3:
                s1_gates(k + 5)
            if not last:
                s_exp(k + 1)
                s2(k + 1)
            if k >= 4:
                copy_f(k - 1)
                copy_i(k - 1)
                if k - 1 < late:
                    copy_oz(k - 1)
                back(k - 1)
            if k == 3:
                for e in range(3):
                    back(e)
            open_sums(k)
            if k == 6:
                pass_1(2, 0, 0, "d")
                pass_1(2, 1, 0, "fP")
            if k < 3:
                if k < 2:
                    pre_d(k + 6)
                move("f", k + 5)
                move("i", k + 5)
                move("rp", k + 5)
                s1_cell(k + 5)
            b_first(k, last)
            if k in (2, 3):
                store_0(k - 2)
            if k == 4:
                back_copy(0, 0, act.copy)
                back_copy(0, 1, act.copy)
            s = raw_at.get(k)
            if s is not None:
                interleave(s, act.copy)
            b_second(k)
            if last:
                break
            v_go(k + 1)
            if k < late:
                v_do(k)
            if k == 5:
                quantize_back(0, 0)
            v_g2(k + 1)
            if k < late:
                v_dz(k)
            if k == 5:
                quantize_back(0, 1)
            if 3 <= k and k - 1 < late:
                if k > 3:
                    store_0(k - 2)
                product_0(k - 1)
            if s is not None and k >= 3:
                quantize_raw(s)
            if k < 3:
                a = k + 5

                def after_d():
                    if a < 7:
                        copies(k)
                        s_abs(a)
                    else:
                        s_ln(4)
                        copies(k)
                        s_ln(5)
                        s_ln(6)
                        s_abs(7)
                        s_ln(7)

                def before_u():
                    quantize_raw(s)
                    if k > 0:
                        product_0(k - 1)

                stage_a(a, after_d, before_u)
                if a == 7:
                    finish_v(7, vec)

        copy_f(7)
        back(7)
        copy_i(7)
        v_do(7)
        v_dz(7)
        pass_1(3, 0, 0, "sum_f")
        pass_1(3, 1, 0, "sum_i")
        back_copy(1, 1, vec.tensor_copy)
        back_copy(1, 0, act.copy)
        store_0(6)
        copy_oz(7)
        quantize_back(1, 1)
        pass_1(2, 0, 1)
        pass_1(2, 1, 1)
        pass_1(3, 0, 1)
        pass_1(3, 1, 1)
        quantize_back(1, 0)
        pass_1(0, 0, 0, "rpP")
        pass_1(0, 0, 1)
        pass_1(0, 1, 0, "iP")
        pass_1(0, 1, 1)
        store_1(2, 0, act.copy)
        store_1(2, 1, vec.tensor_copy)
        product_0(7)
        store_1(3, 0, act.copy)
        pass_1(1, 0, 0, "d")
        pass_1(1, 0, 1)
        pass_1(1, 1, 0, "fP")
        pass_1(1, 1, 1)
        store_1(3, 1, vec.tensor_copy)
        store_1(0, 0, act.copy)
        store_1(0, 1, vec.tensor_copy)
        store_0(7)
        store_1(1, 0, vec.tensor_copy)
        store_1(1, 1, act.copy)
